import numpy as np
import ml_dtypes


def mxq(x, axis, fmt="e4m3"):
    dtype, down = {"e4m3": (ml_dtypes.float8_e4m3fn, 7), "e5m2": (ml_dtypes.float8_e5m2, 14)}[fmt]
    v = np.moveaxis(np.asarray(x, np.float32).astype(ml_dtypes.bfloat16).astype(np.float64), axis, -1)
    blocks = v.reshape(v.shape[:-1] + (-1, 32))
    amax = np.abs(blocks).max(-1, keepdims=True)
    byte = np.maximum(np.where(amax > 0, np.frexp(amax)[1] - 1 + 127, 0) - down, 1)
    scale = np.exp2(byte - 127.0)
    codes = (blocks / scale).astype(np.float32).astype(dtype).astype(np.float64)
    return np.moveaxis((codes * scale).reshape(v.shape), -1, axis)


WIDE = False


def mx_kscale(k):
    if not WIDE:
        return np.ones(k)
    levels = np.array([10, -10, 5, -5, 0])
    a = np.random.permutation(np.resize(levels, k // 512 * 4)).reshape(k // 512, 4)
    idx = np.arange(k)
    return np.exp2(a[idx // 512, idx % 128 // 32])


BF16 = ml_dtypes.bfloat16


def bf(x):
    return np.asarray(x, np.float32).astype(BF16)


def f64(x):
    return np.asarray(x).astype(np.float64)


B, K, O = 512, 2048, 2048

DT = 0.001
TAU_SYN = 0.01
TAU_MEM = 0.005
THRESHOLD = 1.0
ALPHA = float(np.exp(-DT / TAU_SYN))
BETA = float(np.exp(-DT / TAU_MEM))


def spike(v):
    return np.where(v > 0.0, 1.0, 0.0)


def setup_inputs():
    s = mx_kscale(K)
    return {"inputs": bf(np.random.standard_normal((B, K)) * s),
            "I": bf(np.random.standard_normal((B, O))),
            "V": bf(np.random.standard_normal((B, O))),
            "Z": bf(np.where(np.random.random((B, O)) < 0.25, 1.0, 0.0)),
            "fwd_w": bf(np.random.standard_normal((K, O)) * 0.7 / np.sqrt(K) / s[:, None]),
            "rec_w": bf(np.random.standard_normal((O, O)) * 1.4 / np.sqrt(O))}


def reference(inputs, I, V, Z, fwd_w, rec_w):
    z = f64(Z)
    input_current = mxq(f64(inputs), 1, "e4m3") @ mxq(f64(fwd_w), 0, "e4m3")
    rec_current = mxq(z, 1, "e4m3") @ mxq(f64(rec_w), 0, "e4m3")
    is_active = 1.0 - z
    next_I = ALPHA * f64(I) + input_current + rec_current
    next_V = (BETA * f64(V) + next_I) * is_active
    next_Z = spike(next_V - THRESHOLD)
    return next_Z, next_I, next_V

@@ -1,0 +1,243 @@
+import math
+from contextlib import ExitStack
+
+import concourse.bass as bass
+import concourse.mybir as mybir
+import concourse.tile as tile
+from concourse.masks import make_identity
+
+FP8X4 = mybir.dt.float8_e4m3fn_x4
+BF16 = mybir.dt.bfloat16
+F32 = mybir.dt.float32
+U32 = mybir.dt.uint32
+U8 = mybir.dt.uint8
+ALU = mybir.AluOpType
+ACT = mybir.ActivationFunctionType
+
+P = 128
+B, K, O = 512, 2048, 2048
+NT = 512
+N_TILES = O // NT
+M_TILES = B // P
+PASSES = 2 * K // 512
+ALPHA = math.exp(-0.001 / 0.01)
+BETA = math.exp(-0.001 / 0.005)
+FLOPS = 2 * 2 * B * K * O
+MANUAL = True
+EW = 1024
+
+
+def tile_liflayer_kernel(tc, inputs, I, V, Z, fwd_w, rec_w, out_0, out_1, out_2):
+    nc = tc.nc
+    with ExitStack() as ctx:
+        const = ctx.enter_context(tc.tile_pool(name="const", bufs=1))
+        keep = ctx.enter_context(tc.tile_pool(name="keep", bufs=1))
+        big = ctx.enter_context(tc.tile_pool(name="big", bufs=4))
+        grp = ctx.enter_context(tc.tile_pool(name="grp", bufs=6))
+        zout = ctx.enter_context(tc.tile_pool(name="zout", bufs=2))
+        psum = ctx.enter_context(tc.psum_pool(name="psum", bufs=8))
+        if MANUAL:
+            ctx.enter_context(tc.manual_schedule())
+
+        ident = const.tile([P, P], F32, name="ident")
+        make_identity(nc, ident[:])
+        neg_one = const.tile([P, 1], F32, name="neg_one")
+        nc.vector.memset(neg_one[:], -1.0)
+        warm = const.tile([P, 1], F32, name="warm")
+        nc.scalar.activation(out=warm[:], in_=neg_one[:], func=ACT.Sign)
+
+        x_sb = big.tile([P, M_TILES * K], BF16, name="x_sb", tag="big")
+        z_sb = keep.tile([P, M_TILES * K], BF16, name="z_sb")
+        for m in range(M_TILES):
+            nc.sync.dma_start(out=x_sb[:, m * K:(m + 1) * K], in_=inputs[m * P:(m + 1) * P, :])
+        for m in range(M_TILES):
+            nc.sync.dma_start(out=z_sb[:, m * K:(m + 1) * K], in_=Z[m * P:(m + 1) * P, :])
+
+        w_raw = {}
+
+        def load_w(c):
+            src = fwd_w if c < 4 else rec_w
+            r0 = (c % 4) * 512
+            wt = big.tile([P, 4 * O], BF16, name="w_raw%d" % c, tag="big")
+            for u in range(2):
+                nc.sync.dma_start(
+                    out=wt[:, u * 2 * O:(u + 1) * 2 * O],
+                    in_=src[r0 + 256 * u:r0 + 256 * (u + 1), :].rearrange("(q e) c -> q (e c)", e=2),
+                )
+            w_raw[c] = wt
+
+        for c in range(3):
+            load_w(c)
+
+        a_codes = {}
+        a_scales = {}
+
+        def prepare(s, src_sb, mm):
+            srcf = src_sb[:].bitcast(F32)
+            codes = keep.tile([P, 4 * 256], U32, name="a_codes%d%d" % (s, mm), align_bytes=64)
+            scales = keep.tile([P, 4 * 256], U8, name="a_scales%d%d" % (s, mm), align_bytes=64)
+            a_codes[(s, mm)] = codes
+            a_scales[(s, mm)] = scales
+            banks = []
+            for g in range(4):
+                xt = psum.tile([P, NT], F32, name="xt%d%d%d" % (s, mm, g), tag="bank")
+                for u in range(2):
+                    for h in range(2):
+                        m = 2 * mm + h
+                        w0 = m * (K // 2) + 256 * g + 128 * u
+                        nc.tensor.transpose(xt[:, u * 256 + h * P:u * 256 + (h + 1) * P], srcf[:, w0:w0 + P], ident[:])
+                banks.append(xt)
+            gas = []
+            for gp in range(2):
+                ga = grp.tile([P, 2048], BF16, name="ga%d%d%d" % (s, mm, gp), tag="grp", align_bytes=64)
+                gas.append(ga)
+            for g in (0, 2, 1, 3):
+                gaf = gas[g // 2][:].bitcast(F32).rearrange("p (g b u) -> p g b u", g=2, u=2)
+                dst = gaf[:, g % 2, :, :]
+                srcv = banks[g][:].rearrange("p (u b) -> p b u", u=2)
+                if g % 2 == 0:
+                    nc.vector.tensor_copy(out=dst, in_=srcv)
+                else:
+                    nc.scalar.copy(out=dst, in_=srcv)
+            for gp in range(2):
+                nc.vector.quantize_mx(
+                    out=codes[:, gp * 512:(gp + 1) * 512].bitcast(FP8X4),
+                    scales=scales[:, gp * 512:(gp + 1) * 512],
+                    in_=gas[gp][:],
+                )
+
+        prepare(0, x_sb, 0)
+        prepare(0, x_sb, 1)
+        load_w(3)
+        prepare(1, z_sb, 0)
+        prepare(1, z_sb, 1)
+
+        w_codes = {}
+        w_scales = {}
+        w_grp = {}
+
+        def regroup(k, engine):
+            c, n = k // 4, k % 4
+            gw = grp.tile([P, 2048], BF16, name="gw%d" % k, tag="grp", align_bytes=64)
+            dst = gw[:].rearrange("p (c i t) -> p c t i", i=4, t=4)
+            srcv = w_raw[c][:].rearrange("p (t w) -> p t w", t=4)[:, :, n * NT:(n + 1) * NT]
+            srcv = srcv.rearrange("p t (c i) -> p c t i", i=4)
+            if engine == 0:
+                nc.vector.tensor_copy(out=dst, in_=srcv)
+            else:
+                nc.scalar.copy(out=dst, in_=srcv)
+            w_grp[k] = gw
+
+        def quantise(k):
+            codes = keep.tile([P, NT], U32, name="w_codes%d" % k, align_bytes=64)
+            scales = keep.tile([P, NT], U8, name="w_scales%d" % k, align_bytes=64)
+            nc.vector.quantize_mx(out=codes[:].bitcast(FP8X4), scales=scales[:], in_=w_grp[k][:])
+            w_codes[k] = codes
+            w_scales[k] = scales
+
+        acc = {}
+
+        def mx_pass(m, n, c):
+            s, g = c // 4, c % 4
+            col = g * 256 + (m % 2) * P
+            k = 4 * c + n
+            nc.tensor.matmul_mx(
+                out=acc[(m, n)][:],
+                lhsT=a_codes[(s, m // 2)][:, col:col + P].bitcast(FP8X4),
+                lhsT_scale=a_scales[(s, m // 2)][:, col:col + P],
+                rhs=w_codes[k][:].bitcast(FP8X4),
+                rhs_scale=w_scales[k][:],
+                start=(c == 0),
+                stop=(c == PASSES - 1),
+            )
+
+        for m in range(2):
+            for n in range(N_TILES):
+                acc[(m, n)] = psum.tile([P, NT], F32, name="acc%d%d" % (m, n), tag="bank")
+
+        i_sb = None
+        v_sb = None
+
+        def finish_pair(i):
+            for k in (2 * i, 2 * i + 1):
+                quantise(k)
+            for k in (2 * i, 2 * i + 1):
+                for m in range(2):
+                    mx_pass(m, k % 4, k // 4)
+
+        for i in range(16):
+            regroup(2 * i, 0)
+            regroup(2 * i + 1, 1)
+            if i >= 1:
+                finish_pair(i - 1)
+            if i % 2 == 1:
+                c = i // 2
+                if c + 4 < PASSES:
+                    load_w(c + 4)
+                elif c == 5:
+                    i_sb = big.tile([P, M_TILES * O], BF16, name="i_sb", tag="big")
+                    v_sb = big.tile([P, M_TILES * O], BF16, name="v_sb", tag="big")
+                    for m in range(M_TILES):
+                        nc.sync.dma_start(out=i_sb[:, m * O:(m + 1) * O], in_=I[m * P:(m + 1) * P, :])
+                        nc.sync.dma_start(out=v_sb[:, m * O:(m + 1) * O], in_=V[m * P:(m + 1) * P, :])
+        finish_pair(15)
+
+        outs = {}
+
+        def current(m):
+            ot = big.tile([P, 2 * O], F32, name="ot%d" % m, tag="big")
+            outs[m] = ot
+            for n in range(N_TILES):
+                nc.vector.scalar_tensor_tensor(
+                    out=ot[:, n * NT:(n + 1) * NT],
+                    in0=i_sb[:, m * O + n * NT:m * O + (n + 1) * NT],
+                    scalar=ALPHA,
+                    in1=acc[(m, n)][:],
+                    op0=ALU.mult,
+                    op1=ALU.add,
+                )
+            nc.sync.dma_start(out=out_1[m * P:(m + 1) * P, :], in_=ot[:, 0:O])
+
+        def membrane(m):
+            ot = outs[m]
+            zt = zout.tile([P, O], F32, name="zt%d" % m, tag="zt")
+            for e in range(O // EW):
+                cols = slice(e * EW, (e + 1) * EW)
+                nv = ot[:, O + e * EW:O + (e + 1) * EW]
+                nc.vector.scalar_tensor_tensor(
+                    out=nv,
+                    in0=v_sb[:, m * O + e * EW:m * O + (e + 1) * EW],
+                    scalar=-BETA,
+                    in1=ot[:, cols],
+                    op0=ALU.mult,
+                    op1=ALU.subtract,
+                )
+                nc.vector.scalar_tensor_tensor(
+                    out=nv,
+                    in0=z_sb[:, m * O + e * EW:m * O + (e + 1) * EW],
+                    scalar=1.0,
+                    in1=nv,
+                    op0=ALU.subtract,
+                    op1=ALU.mult,
+                )
+                nc.scalar.activation(out=zt[:, cols], in_=nv, func=ACT.Relu, bias=neg_one[:], scale=1.0)
+                nc.scalar.activation(out=zt[:, cols], in_=zt[:, cols], func=ACT.Sign)
+            nc.sync.dma_start(out=out_2[m * P:(m + 1) * P, :], in_=ot[:, O:2 * O])
+            nc.sync.dma_start(out=out_0[m * P:(m + 1) * P, :], in_=zt[:])
+
+        def second_half(m):
+            for n in range(N_TILES):
+                acc[(m, n)] = psum.tile([P, NT], F32, name="acc%d%d" % (m, n), tag="bank")
+                for c in range(PASSES):
+                    mx_pass(m, n, c)
+
+        current(0)
+        second_half(2)
+        membrane(0)
+        current(1)
+        second_half(3)
+        membrane(1)
+        current(2)
+        membrane(2)
+        current(3)
+        membrane(3)

@@ -1,9 +1,7 @@
 import math
 from contextlib import ExitStack
 
-import concourse.bass as bass
 import concourse.mybir as mybir
-import concourse.tile as tile
 from concourse.masks import make_identity
 
 FP8X4 = mybir.dt.float8_e4m3fn_x4
@@ -17,14 +15,19 @@ ACT = mybir.ActivationFunctionType
 P = 128
 B, K, O = 512, 2048, 2048
 NT = 512
-N_TILES = O // NT
+HW = 1024
 M_TILES = B // P
 PASSES = 2 * K // 512
+LAST = PASSES - 1
 ALPHA = math.exp(-0.001 / 0.01)
 BETA = math.exp(-0.001 / 0.005)
 FLOPS = 2 * 2 * B * K * O
-MANUAL = True
-EW = 1024
+ORDER = ("w0", "x", "w1", "z", "w2", "w3", "w4", "w5", "w6", "w7")
+V_EXITS = (0,)
+BIG_BUFS = 4
+GRP_BUFS = 3
+OUT_BUFS = 2
+IV_ORDER = (("i", 0), ("i", 1), ("v", 0), ("i", 2), ("v", 1), ("i", 3), ("v", 2), ("v", 3))
 
 
 def tile_liflayer_kernel(tc, inputs, I, V, Z, fwd_w, rec_w, out_0, out_1, out_2):
@@ -32,12 +35,11 @@ def tile_liflayer_kernel(tc, inputs, I, V, Z, fwd_w, rec_w, out_0, out_1, out_2)
     with ExitStack() as ctx:
         const = ctx.enter_context(tc.tile_pool(name="const", bufs=1))
         keep = ctx.enter_context(tc.tile_pool(name="keep", bufs=1))
-        big = ctx.enter_context(tc.tile_pool(name="big", bufs=4))
-        grp = ctx.enter_context(tc.tile_pool(name="grp", bufs=6))
-        zout = ctx.enter_context(tc.tile_pool(name="zout", bufs=2))
+        big = ctx.enter_context(tc.tile_pool(name="big", bufs=BIG_BUFS))
+        grp = ctx.enter_context(tc.tile_pool(name="grp", bufs=GRP_BUFS))
+        outp = ctx.enter_context(tc.tile_pool(name="outp", bufs=OUT_BUFS))
         psum = ctx.enter_context(tc.psum_pool(name="psum", bufs=8))
-        if MANUAL:
-            ctx.enter_context(tc.manual_schedule())
+        ctx.enter_context(tc.manual_schedule())
 
         ident = const.tile([P, P], F32, name="ident")
         make_identity(nc, ident[:])
@@ -46,198 +48,224 @@ def tile_liflayer_kernel(tc, inputs, I, V, Z, fwd_w, rec_w, out_0, out_1, out_2)
         warm = const.tile([P, 1], F32, name="warm")
         nc.scalar.activation(out=warm[:], in_=neg_one[:], func=ACT.Sign)
 
-        x_sb = big.tile([P, M_TILES * K], BF16, name="x_sb", tag="big")
-        z_sb = keep.tile([P, M_TILES * K], BF16, name="z_sb")
-        for m in range(M_TILES):
-            nc.sync.dma_start(out=x_sb[:, m * K:(m + 1) * K], in_=inputs[m * P:(m + 1) * P, :])
-        for m in range(M_TILES):
-            nc.sync.dma_start(out=z_sb[:, m * K:(m + 1) * K], in_=Z[m * P:(m + 1) * P, :])
+        raw = {}
 
-        w_raw = {}
-
-        def load_w(c):
+        def load_w(c, h0, h1, name):
             src = fwd_w if c < 4 else rec_w
             r0 = (c % 4) * 512
-            wt = big.tile([P, 4 * O], BF16, name="w_raw%d" % c, tag="big")
+            wid = (h1 - h0) * HW
+            t = big.tile([P, 4 * wid], BF16, name=name, tag="big")
+            raw[name] = t
+            tv = t[:].rearrange("p (t w) -> p t w", t=4)
             for u in range(2):
                 nc.sync.dma_start(
-                    out=wt[:, u * 2 * O:(u + 1) * 2 * O],
-                    in_=src[r0 + 256 * u:r0 + 256 * (u + 1), :].rearrange("(q e) c -> q (e c)", e=2),
+                    out=tv[:, 2 * u:2 * u + 2, :],
+                    in_=src[r0 + 256 * u:r0 + 256 * (u + 1), h0 * HW:h1 * HW].rearrange("(q e) c -> q e c", e=2),
                 )
-            w_raw[c] = wt
 
-        for c in range(3):
-            load_w(c)
+        def load_rows(t, src, m):
+            nc.sync.dma_start(out=t[:, m * K:(m + 1) * K], in_=src[m * P:(m + 1) * P, :])
+
+        def load(item):
+            if item == "w%d" % LAST:
+                load_w(LAST, 0, 1, "w%da" % LAST)
+            elif item == "w%db" % LAST:
+                load_w(LAST, 1, 2, item)
+            elif item[0] == "w":
+                load_w(int(item[1:]), 0, 2, item)
+            elif item == "iv":
+                raw["i"] = big.tile([P, M_TILES * O], BF16, name="i_sb", tag="big")
+                raw["v"] = big.tile([P, M_TILES * O], BF16, name="v_sb", tag="big")
+                for which, m in IV_ORDER:
+                    load_rows(raw[which], I if which == "i" else V, m)
+            else:
+                if item == "z":
+                    raw[item] = keep.tile([P, M_TILES * K], BF16, name="z_sb")
+                else:
+                    raw[item] = big.tile([P, M_TILES * K], BF16, name="x_sb", tag="big")
+                for m in range(M_TILES):
+                    load_rows(raw[item], inputs if item == "x" else Z, m)
 
         a_codes = {}
         a_scales = {}
+        w_codes = {}
+        w_scales = {}
+        acc = {}
+        pending = []
+        pe_backlog = []
+        state = {"acts": 0}
 
-        def prepare(s, src_sb, mm):
-            srcf = src_sb[:].bitcast(F32)
+        def mx_pass(m, n, c):
+            s, g = c // 4, c % 4
+            col = g * 256 + (m % 2) * P
+            j = 2 * c + n // 2
+            wcol = (n % 2) * NT
+            nc.tensor.matmul_mx(
+                out=acc[(m, n)][:],
+                lhsT=a_codes[(s, m // 2)][:, col:col + P].bitcast(FP8X4),
+                lhsT_scale=a_scales[(s, m // 2)][:, col:col + P],
+                rhs=w_codes[j][:, wcol:wcol + NT].bitcast(FP8X4),
+                rhs_scale=w_scales[j][:, wcol:wcol + NT],
+                start=(c == 0),
+                stop=(c == LAST),
+            )
+
+        def first_half_passes(c):
+            for n in range(2):
+                for m in range(M_TILES):
+                    mx_pass(m, n, c)
+
+        def flush():
+            while pending:
+                pending.pop(0)()
+
+        def act_step(s, mm):
+            srcf = raw["x" if s == 0 else "z"][:].bitcast(F32)
             codes = keep.tile([P, 4 * 256], U32, name="a_codes%d%d" % (s, mm), align_bytes=64)
             scales = keep.tile([P, 4 * 256], U8, name="a_scales%d%d" % (s, mm), align_bytes=64)
             a_codes[(s, mm)] = codes
             a_scales[(s, mm)] = scales
+            ga = grp.tile([P, 4096], BF16, name="ga%d%d" % (s, mm), tag="grp", align_bytes=64)
+            gaf = ga[:].bitcast(F32).rearrange("p (g b u) -> p g b u", g=4, u=2)
             banks = []
             for g in range(4):
                 xt = psum.tile([P, NT], F32, name="xt%d%d%d" % (s, mm, g), tag="bank")
                 for u in range(2):
                     for h in range(2):
-                        m = 2 * mm + h
-                        w0 = m * (K // 2) + 256 * g + 128 * u
+                        w0 = (2 * mm + h) * (K // 2) + 256 * g + 128 * u
                         nc.tensor.transpose(xt[:, u * 256 + h * P:u * 256 + (h + 1) * P], srcf[:, w0:w0 + P], ident[:])
                 banks.append(xt)
-            gas = []
-            for gp in range(2):
-                ga = grp.tile([P, 2048], BF16, name="ga%d%d%d" % (s, mm, gp), tag="grp", align_bytes=64)
-                gas.append(ga)
-            for g in (0, 2, 1, 3):
-                gaf = gas[g // 2][:].bitcast(F32).rearrange("p (g b u) -> p g b u", g=2, u=2)
-                dst = gaf[:, g % 2, :, :]
+            for g in range(4):
                 srcv = banks[g][:].rearrange("p (u b) -> p b u", u=2)
-                if g % 2 == 0:
+                if g in V_EXITS:
+                    nc.vector.tensor_copy(out=gaf[:, g, :, :], in_=srcv)
+                else:
+                    nc.scalar.copy(out=gaf[:, g, :, :], in_=srcv)
+            flush()
+
+            def finish():
+                nc.vector.quantize_mx(out=codes[:].bitcast(FP8X4), scales=scales[:], in_=ga[:])
+                state["acts"] += 1
+                if state["acts"] == 4:
+                    for n in range(2):
+                        for m in range(M_TILES):
+                            acc[(m, n)] = psum.tile([P, NT], F32, name="acc%d%d" % (m, n), tag="bank")
+                    while pe_backlog:
+                        first_half_passes(pe_backlog.pop(0))
+            pending.append(finish)
+
+        def w_step(j, engines):
+            c, h = j // 2, j % 2
+            gw = grp.tile([P, 4096], BF16, name="gw%d" % j, tag="grp", align_bytes=64)
+            if c == LAST:
+                rv = raw["w%d%s" % (c, "ab"[h])][:].rearrange("p (t w) -> p t w", t=4)
+                base = 0
+            else:
+                rv = raw["w%d" % c][:].rearrange("p (t w) -> p t w", t=4)
+                base = h * HW
+            for e in range(2):
+                dst = gw[:, e * 2048:(e + 1) * 2048].rearrange("p (c i t) -> p c t i", i=4, t=4)
+                srcv = rv[:, :, base + e * NT:base + (e + 1) * NT].rearrange("p t (c i) -> p c t i", i=4)
+                if engines[e] == "v":
                     nc.vector.tensor_copy(out=dst, in_=srcv)
                 else:
                     nc.scalar.copy(out=dst, in_=srcv)
-            for gp in range(2):
-                nc.vector.quantize_mx(
-                    out=codes[:, gp * 512:(gp + 1) * 512].bitcast(FP8X4),
-                    scales=scales[:, gp * 512:(gp + 1) * 512],
-                    in_=gas[gp][:],
-                )
+            flush()
 
-        prepare(0, x_sb, 0)
-        prepare(0, x_sb, 1)
-        load_w(3)
-        prepare(1, z_sb, 0)
-        prepare(1, z_sb, 1)
+            def finish():
+                codes = keep.tile([P, 2 * NT], U32, name="w_codes%d" % j, align_bytes=64)
+                scales = keep.tile([P, 2 * NT], U8, name="w_scales%d" % j, align_bytes=64)
+                w_codes[j] = codes
+                w_scales[j] = scales
+                nc.vector.quantize_mx(out=codes[:].bitcast(FP8X4), scales=scales[:], in_=gw[:])
+                if h == 0:
+                    if state["acts"] == 4:
+                        first_half_passes(c)
+                    else:
+                        pe_backlog.append(c)
+            pending.append(finish)
 
-        w_codes = {}
-        w_scales = {}
-        w_grp = {}
-
-        def regroup(k, engine):
-            c, n = k // 4, k % 4
-            gw = grp.tile([P, 2048], BF16, name="gw%d" % k, tag="grp", align_bytes=64)
-            dst = gw[:].rearrange("p (c i t) -> p c t i", i=4, t=4)
-            srcv = w_raw[c][:].rearrange("p (t w) -> p t w", t=4)[:, :, n * NT:(n + 1) * NT]
-            srcv = srcv.rearrange("p t (c i) -> p c t i", i=4)
-            if engine == 0:
-                nc.vector.tensor_copy(out=dst, in_=srcv)
+        loads = list(ORDER) + ["w%db" % LAST, None, "iv"]
+        ahead = BIG_BUFS + 1
+        for item in loads[:ahead]:
+            load(item)
+        nxt = ahead
+        for item in ORDER:
+            if item == "w%d" % LAST:
+                w_step(2 * LAST, "vs")
+                flush()
+                w_step(2 * LAST + 1, "ss")
+            elif item[0] == "w":
+                c = int(item[1:])
+                w_step(2 * c, "vs")
+                w_step(2 * c + 1, "vs")
             else:
-                nc.scalar.copy(out=dst, in_=srcv)
-            w_grp[k] = gw
+                s = 0 if item == "x" else 1
+                act_step(s, 0)
+                act_step(s, 1)
+            if item != "z" and nxt < len(loads):
+                if loads[nxt] is not None:
+                    load(loads[nxt])
+                nxt += 1
+        i_sb = raw["i"]
+        v_sb = raw["v"]
+        z_sb = raw["z"]
 
-        def quantise(k):
-            codes = keep.tile([P, NT], U32, name="w_codes%d" % k, align_bytes=64)
-            scales = keep.tile([P, NT], U8, name="w_scales%d" % k, align_bytes=64)
-            nc.vector.quantize_mx(out=codes[:].bitcast(FP8X4), scales=scales[:], in_=w_grp[k][:])
-            w_codes[k] = codes
-            w_scales[k] = scales
+        n_i = {}
 
-        acc = {}
+        late = []
 
-        def mx_pass(m, n, c):
-            s, g = c // 4, c % 4
-            col = g * 256 + (m % 2) * P
-            k = 4 * c + n
-            nc.tensor.matmul_mx(
-                out=acc[(m, n)][:],
-                lhsT=a_codes[(s, m // 2)][:, col:col + P].bitcast(FP8X4),
-                lhsT_scale=a_scales[(s, m // 2)][:, col:col + P],
-                rhs=w_codes[k][:].bitcast(FP8X4),
-                rhs_scale=w_scales[k][:],
-                start=(c == 0),
-                stop=(c == PASSES - 1),
-            )
+        def late_stores(keep_n):
+            while len(late) > keep_n:
+                dst, srcv = late.pop(0)
+                nc.sync.dma_start(out=dst, in_=srcv)
 
-        for m in range(2):
-            for n in range(N_TILES):
-                acc[(m, n)] = psum.tile([P, NT], F32, name="acc%d%d" % (m, n), tag="bank")
-
-        i_sb = None
-        v_sb = None
-
-        def finish_pair(i):
-            for k in (2 * i, 2 * i + 1):
-                quantise(k)
-            for k in (2 * i, 2 * i + 1):
-                for m in range(2):
-                    mx_pass(m, k % 4, k // 4)
-
-        for i in range(16):
-            regroup(2 * i, 0)
-            regroup(2 * i + 1, 1)
-            if i >= 1:
-                finish_pair(i - 1)
-            if i % 2 == 1:
-                c = i // 2
-                if c + 4 < PASSES:
-                    load_w(c + 4)
-                elif c == 5:
-                    i_sb = big.tile([P, M_TILES * O], BF16, name="i_sb", tag="big")
-                    v_sb = big.tile([P, M_TILES * O], BF16, name="v_sb", tag="big")
-                    for m in range(M_TILES):
-                        nc.sync.dma_start(out=i_sb[:, m * O:(m + 1) * O], in_=I[m * P:(m + 1) * P, :])
-                        nc.sync.dma_start(out=v_sb[:, m * O:(m + 1) * O], in_=V[m * P:(m + 1) * P, :])
-        finish_pair(15)
-
-        outs = {}
-
-        def current(m):
-            ot = big.tile([P, 2 * O], F32, name="ot%d" % m, tag="big")
-            outs[m] = ot
-            for n in range(N_TILES):
+        def current(m, h):
+            t = outp.tile([P, HW], F32, name="ni%d%d" % (m, h), tag="ni")
+            n_i[(m, h)] = t
+            for e in range(2):
+                c0 = m * O + h * HW + e * NT
                 nc.vector.scalar_tensor_tensor(
-                    out=ot[:, n * NT:(n + 1) * NT],
-                    in0=i_sb[:, m * O + n * NT:m * O + (n + 1) * NT],
-                    scalar=ALPHA,
-                    in1=acc[(m, n)][:],
-                    op0=ALU.mult,
-                    op1=ALU.add,
-                )
-            nc.sync.dma_start(out=out_1[m * P:(m + 1) * P, :], in_=ot[:, 0:O])
+                    out=t[:, e * NT:(e + 1) * NT], in0=i_sb[:, c0:c0 + NT], scalar=ALPHA,
+                    in1=acc[(m, 2 * h + e)][:], op0=ALU.mult, op1=ALU.add)
+            nc.sync.dma_start(out=out_1[m * P:(m + 1) * P, h * HW:(h + 1) * HW], in_=t[:])
+            late_stores(0)
 
-        def membrane(m):
-            ot = outs[m]
-            zt = zout.tile([P, O], F32, name="zt%d" % m, tag="zt")
-            for e in range(O // EW):
-                cols = slice(e * EW, (e + 1) * EW)
-                nv = ot[:, O + e * EW:O + (e + 1) * EW]
+        def membrane(m, h, pieces, on_vector):
+            nv = outp.tile([P, HW], F32, name="nv%d%d" % (m, h), tag="nv")
+            nz = outp.tile([P, HW], F32, name="nz%d%d" % (m, h), tag="nz")
+            rows = slice(m * P, (m + 1) * P)
+            wid = HW // pieces
+            for e in range(pieces):
+                cs = slice(e * wid, (e + 1) * wid)
+                c0 = m * O + h * HW + e * wid
                 nc.vector.scalar_tensor_tensor(
-                    out=nv,
-                    in0=v_sb[:, m * O + e * EW:m * O + (e + 1) * EW],
-                    scalar=-BETA,
-                    in1=ot[:, cols],
-                    op0=ALU.mult,
-                    op1=ALU.subtract,
-                )
+                    out=nv[:, cs], in0=v_sb[:, c0:c0 + wid], scalar=-BETA,
+                    in1=n_i[(m, h)][:, cs], op0=ALU.mult, op1=ALU.subtract)
                 nc.vector.scalar_tensor_tensor(
-                    out=nv,
-                    in0=z_sb[:, m * O + e * EW:m * O + (e + 1) * EW],
-                    scalar=1.0,
-                    in1=nv,
-                    op0=ALU.subtract,
-                    op1=ALU.mult,
-                )
-                nc.scalar.activation(out=zt[:, cols], in_=nv, func=ACT.Relu, bias=neg_one[:], scale=1.0)
-                nc.scalar.activation(out=zt[:, cols], in_=zt[:, cols], func=ACT.Sign)
-            nc.sync.dma_start(out=out_2[m * P:(m + 1) * P, :], in_=ot[:, O:2 * O])
-            nc.sync.dma_start(out=out_0[m * P:(m + 1) * P, :], in_=zt[:])
+                    out=nv[:, cs], in0=z_sb[:, c0:c0 + wid], scalar=1.0,
+                    in1=nv[:, cs], op0=ALU.subtract, op1=ALU.mult)
+                if on_vector and e == pieces - 1:
+                    nc.vector.tensor_scalar(out=nz[:, cs], in0=nv[:, cs], scalar1=1.0, scalar2=None, op0=ALU.is_gt)
+                else:
+                    nc.scalar.activation(out=nz[:, cs], in_=nv[:, cs], func=ACT.Relu, bias=neg_one[:], scale=1.0)
+                    nc.scalar.activation(out=nz[:, cs], in_=nz[:, cs], func=ACT.Sign)
+                d0 = h * HW + e * wid
+                nc.sync.dma_start(out=out_2[rows, d0:d0 + wid], in_=nv[:, cs])
+                late.append((out_0[rows, d0:d0 + wid], nz[:, cs]))
 
         def second_half(m):
-            for n in range(N_TILES):
+            for n in (2, 3):
                 acc[(m, n)] = psum.tile([P, NT], F32, name="acc%d%d" % (m, n), tag="bank")
                 for c in range(PASSES):
                     mx_pass(m, n, c)
 
-        current(0)
-        second_half(2)
-        membrane(0)
-        current(1)
-        second_half(3)
-        membrane(1)
-        current(2)
-        membrane(2)
-        current(3)
-        membrane(3)
+        for m in range(M_TILES):
+            current(m, 0)
+            membrane(m, 0, 1, False)
+            flush()
+            second_half(m)
+        for m in range(M_TILES):
+            current(m, 1)
+            membrane(m, 1, 1, m == M_TILES - 1)
+        late_stores(0)

@@ -25,9 +25,8 @@ FLOPS = 2 * 2 * B * K * O
 ORDER = ("w0", "x", "w1", "z", "w2", "w3", "w4", "w5", "w6", "w7")
 V_EXITS = (0,)
 BIG_BUFS = 4
-GRP_BUFS = 3
-OUT_BUFS = 2
-IV_ORDER = (("i", 0), ("i", 1), ("v", 0), ("i", 2), ("v", 1), ("i", 3), ("v", 2), ("v", 3))
+GRP_BUFS = 6
+LAST_PIECES = (1024,)
 
 
 def tile_liflayer_kernel(tc, inputs, I, V, Z, fwd_w, rec_w, out_0, out_1, out_2):
@@ -37,7 +36,6 @@ def tile_liflayer_kernel(tc, inputs, I, V, Z, fwd_w, rec_w, out_0, out_1, out_2)
         keep = ctx.enter_context(tc.tile_pool(name="keep", bufs=1))
         big = ctx.enter_context(tc.tile_pool(name="big", bufs=BIG_BUFS))
         grp = ctx.enter_context(tc.tile_pool(name="grp", bufs=GRP_BUFS))
-        outp = ctx.enter_context(tc.tile_pool(name="outp", bufs=OUT_BUFS))
         psum = ctx.enter_context(tc.psum_pool(name="psum", bufs=8))
         ctx.enter_context(tc.manual_schedule())
 
@@ -50,41 +48,42 @@ def tile_liflayer_kernel(tc, inputs, I, V, Z, fwd_w, rec_w, out_0, out_1, out_2)
 
         raw = {}
 
-        def load_w(c, h0, h1, name):
+        def load_w(c):
             src = fwd_w if c < 4 else rec_w
             r0 = (c % 4) * 512
-            wid = (h1 - h0) * HW
-            t = big.tile([P, 4 * wid], BF16, name=name, tag="big")
-            raw[name] = t
-            tv = t[:].rearrange("p (t w) -> p t w", t=4)
-            for u in range(2):
-                nc.sync.dma_start(
-                    out=tv[:, 2 * u:2 * u + 2, :],
-                    in_=src[r0 + 256 * u:r0 + 256 * (u + 1), h0 * HW:h1 * HW].rearrange("(q e) c -> q e c", e=2),
-                )
+            t = big.tile([P, 4 * O], BF16, name="w%d" % c, tag="big")
+            raw["w%d" % c] = t
+            halves = 2 if c == LAST else 1
+            wid = O // halves
+            for h in range(halves):
+                tv = t[:, h * 4 * wid:(h + 1) * 4 * wid].rearrange("p (t w) -> p t w", t=4)
+                for u in range(2):
+                    nc.sync.dma_start(
+                        out=tv[:, 2 * u:2 * u + 2, :],
+                        in_=src[r0 + 256 * u:r0 + 256 * (u + 1), h * wid:(h + 1) * wid].rearrange(
+                            "(q e) c -> q e c", e=2),
+                    )
 
-        def load_rows(t, src, m):
-            nc.sync.dma_start(out=t[:, m * K:(m + 1) * K], in_=src[m * P:(m + 1) * P, :])
+        def load_rows(t, src, mm):
+            nc.sync.dma_start(out=t[:, 2 * mm * K:2 * (mm + 1) * K],
+                              in_=src.rearrange("(p j) k -> p (j k)", j=M_TILES)[:, 2 * mm * K:2 * (mm + 1) * K])
 
         def load(item):
-            if item == "w%d" % LAST:
-                load_w(LAST, 0, 1, "w%da" % LAST)
-            elif item == "w%db" % LAST:
-                load_w(LAST, 1, 2, item)
-            elif item[0] == "w":
-                load_w(int(item[1:]), 0, 2, item)
+            if item[0] == "w":
+                load_w(int(item[1:]))
             elif item == "iv":
                 raw["i"] = big.tile([P, M_TILES * O], BF16, name="i_sb", tag="big")
                 raw["v"] = big.tile([P, M_TILES * O], BF16, name="v_sb", tag="big")
-                for which, m in IV_ORDER:
-                    load_rows(raw[which], I if which == "i" else V, m)
+                for mm in range(2):
+                    load_rows(raw["i"], I, mm)
+                    load_rows(raw["v"], V, mm)
             else:
                 if item == "z":
                     raw[item] = keep.tile([P, M_TILES * K], BF16, name="z_sb")
                 else:
                     raw[item] = big.tile([P, M_TILES * K], BF16, name="x_sb", tag="big")
-                for m in range(M_TILES):
-                    load_rows(raw[item], inputs if item == "x" else Z, m)
+                for mm in range(2):
+                    load_rows(raw[item], inputs if item == "x" else Z, mm)
 
         a_codes = {}
         a_scales = {}
@@ -93,6 +92,7 @@ def tile_liflayer_kernel(tc, inputs, I, V, Z, fwd_w, rec_w, out_0, out_1, out_2)
         acc = {}
         pending = []
         pe_backlog = []
+        split = []
         state = {"acts": 0}
 
         def mx_pass(m, n, c):
@@ -110,9 +110,9 @@ def tile_liflayer_kernel(tc, inputs, I, V, Z, fwd_w, rec_w, out_0, out_1, out_2)
                 stop=(c == LAST),
             )
 
-        def first_half_passes(c):
-            for n in range(2):
-                for m in range(M_TILES):
+        def first_half_passes(c, ms):
+            for m in ms:
+                for n in range(2):
                     mx_pass(m, n, c)
 
         def flush():
@@ -151,14 +151,14 @@ def tile_liflayer_kernel(tc, inputs, I, V, Z, fwd_w, rec_w, out_0, out_1, out_2)
                         for m in range(M_TILES):
                             acc[(m, n)] = psum.tile([P, NT], F32, name="acc%d%d" % (m, n), tag="bank")
                     while pe_backlog:
-                        first_half_passes(pe_backlog.pop(0))
+                        first_half_passes(pe_backlog.pop(0), (0, 1, 2, 3))
             pending.append(finish)
 
         def w_step(j, engines):
             c, h = j // 2, j % 2
             gw = grp.tile([P, 4096], BF16, name="gw%d" % j, tag="grp", align_bytes=64)
             if c == LAST:
-                rv = raw["w%d%s" % (c, "ab"[h])][:].rearrange("p (t w) -> p t w", t=4)
+                rv = raw["w%d" % c][:, h * 4 * HW:(h + 1) * 4 * HW].rearrange("p (t w) -> p t w", t=4)
                 base = 0
             else:
                 rv = raw["w%d" % c][:].rearrange("p (t w) -> p t w", t=4)
@@ -178,14 +178,20 @@ def tile_liflayer_kernel(tc, inputs, I, V, Z, fwd_w, rec_w, out_0, out_1, out_2)
                 w_codes[j] = codes
                 w_scales[j] = scales
                 nc.vector.quantize_mx(out=codes[:].bitcast(FP8X4), scales=scales[:], in_=gw[:])
-                if h == 0:
-                    if state["acts"] == 4:
-                        first_half_passes(c)
-                    else:
+                if state["acts"] < 4:
+                    if h == 0:
                         pe_backlog.append(c)
+                elif c == LAST:
+                    if h == 0:
+                        first_half_passes(c, (0, 1, 2, 3))
+                elif c in split:
+                    first_half_passes(c, (2, 3))
+                elif h == 0:
+                    first_half_passes(c, (0, 1))
+                    split.append(c)
             pending.append(finish)
 
-        loads = list(ORDER) + ["w%db" % LAST, None, "iv"]
+        loads = list(ORDER) + [None, "iv"]
         ahead = BIG_BUFS + 1
         for item in loads[:ahead]:
             load(item)
@@ -211,48 +217,56 @@ def tile_liflayer_kernel(tc, inputs, I, V, Z, fwd_w, rec_w, out_0, out_1, out_2)
         v_sb = raw["v"]
         z_sb = raw["z"]
 
-        n_i = {}
-
+        o_view = [o.rearrange("(p j) c -> p j c", j=M_TILES) for o in (out_0, out_1, out_2)]
+        pair = {}
+        spikes = {}
         late = []
 
-        def late_stores(keep_n):
-            while len(late) > keep_n:
+        def late_stores():
+            while late:
                 dst, srcv = late.pop(0)
                 nc.sync.dma_start(out=dst, in_=srcv)
 
-        def current(m, h):
-            t = outp.tile([P, HW], F32, name="ni%d%d" % (m, h), tag="ni")
-            n_i[(m, h)] = t
+        def current(k):
+            m, h = k % M_TILES, k // M_TILES
+            t = grp.tile([P, 2 * HW], F32, name="pair%d" % k, tag="grp", align_bytes=64)
+            pair[k] = t
             for e in range(2):
                 c0 = m * O + h * HW + e * NT
                 nc.vector.scalar_tensor_tensor(
                     out=t[:, e * NT:(e + 1) * NT], in0=i_sb[:, c0:c0 + NT], scalar=ALPHA,
                     in1=acc[(m, 2 * h + e)][:], op0=ALU.mult, op1=ALU.add)
-            nc.sync.dma_start(out=out_1[m * P:(m + 1) * P, h * HW:(h + 1) * HW], in_=t[:])
-            late_stores(0)
+            nc.sync.dma_start(out=o_view[1][:, m, h * HW:(h + 1) * HW], in_=t[:, 0:HW])
+            late_stores()
 
-        def membrane(m, h, pieces, on_vector):
-            nv = outp.tile([P, HW], F32, name="nv%d%d" % (m, h), tag="nv")
-            nz = outp.tile([P, HW], F32, name="nz%d%d" % (m, h), tag="nz")
-            rows = slice(m * P, (m + 1) * P)
-            wid = HW // pieces
-            for e in range(pieces):
-                cs = slice(e * wid, (e + 1) * wid)
-                c0 = m * O + h * HW + e * wid
+        def membrane(k, widths, on_vector):
+            m, h = k % M_TILES, k // M_TILES
+            t = pair[k]
+            if k % 2 == 0:
+                spikes[k // 2] = grp.tile([P, 2 * HW], F32, name="spikes%d" % (k // 2), tag="grp", align_bytes=64)
+            zt = spikes[k // 2]
+            z0 = (k % 2) * HW
+            a = 0
+            for e, wid in enumerate(widths):
+                c0 = m * O + h * HW + a
+                ni = t[:, a:a + wid]
+                nv = t[:, HW + a:HW + a + wid]
+                nz = zt[:, z0 + a:z0 + a + wid]
                 nc.vector.scalar_tensor_tensor(
-                    out=nv[:, cs], in0=v_sb[:, c0:c0 + wid], scalar=-BETA,
-                    in1=n_i[(m, h)][:, cs], op0=ALU.mult, op1=ALU.subtract)
+                    out=nv, in0=v_sb[:, c0:c0 + wid], scalar=-BETA, in1=ni, op0=ALU.mult, op1=ALU.subtract)
                 nc.vector.scalar_tensor_tensor(
-                    out=nv[:, cs], in0=z_sb[:, c0:c0 + wid], scalar=1.0,
-                    in1=nv[:, cs], op0=ALU.subtract, op1=ALU.mult)
-                if on_vector and e == pieces - 1:
-                    nc.vector.tensor_scalar(out=nz[:, cs], in0=nv[:, cs], scalar1=1.0, scalar2=None, op0=ALU.is_gt)
+                    out=nv, in0=z_sb[:, c0:c0 + wid], scalar=1.0, in1=nv, op0=ALU.subtract, op1=ALU.mult)
+                if on_vector and e == len(widths) - 1:
+                    nc.vector.tensor_scalar(out=nz, in0=nv, scalar1=1.0, scalar2=None, op0=ALU.is_gt)
                 else:
-                    nc.scalar.activation(out=nz[:, cs], in_=nv[:, cs], func=ACT.Relu, bias=neg_one[:], scale=1.0)
-                    nc.scalar.activation(out=nz[:, cs], in_=nz[:, cs], func=ACT.Sign)
-                d0 = h * HW + e * wid
-                nc.sync.dma_start(out=out_2[rows, d0:d0 + wid], in_=nv[:, cs])
-                late.append((out_0[rows, d0:d0 + wid], nz[:, cs]))
+                    nc.scalar.activation(out=nz, in_=nv, func=ACT.Relu, bias=neg_one[:], scale=1.0)
+                    nc.scalar.activation(out=nz, in_=nz, func=ACT.Sign)
+                d0 = h * HW + a
+                nc.sync.dma_start(out=o_view[2][:, m, d0:d0 + wid], in_=nv)
+                if len(widths) > 1:
+                    late_stores()
+                late.append((o_view[0][:, m, d0:d0 + wid], nz))
+                a += wid
 
         def second_half(m):
             for n in (2, 3):
@@ -260,12 +274,13 @@ def tile_liflayer_kernel(tc, inputs, I, V, Z, fwd_w, rec_w, out_0, out_1, out_2)
                 for c in range(PASSES):
                     mx_pass(m, n, c)
 
-        for m in range(M_TILES):
-            current(m, 0)
-            membrane(m, 0, 1, False)
-            flush()
-            second_half(m)
-        for m in range(M_TILES):
-            current(m, 1)
-            membrane(m, 1, 1, m == M_TILES - 1)
-        late_stores(0)
+        for k in range(2 * M_TILES):
+            current(k)
+            if k == 2 * M_TILES - 1:
+                membrane(k, LAST_PIECES, True)
+            else:
+                membrane(k, (HW,), False)
+            if k < M_TILES:
+                flush()
+                second_half(k)
+        late_stores()

@@ -26,7 +26,6 @@ ORDER = ("w0", "x", "w1", "z", "w2", "w3", "w4", "w5", "w6", "w7")
 V_EXITS = (0,)
 BIG_BUFS = 4
 GRP_BUFS = 6
-LAST_PIECES = (1024,)
 
 
 def tile_liflayer_kernel(tc, inputs, I, V, Z, fwd_w, rec_w, out_0, out_1, out_2):
@@ -239,34 +238,36 @@ def tile_liflayer_kernel(tc, inputs, I, V, Z, fwd_w, rec_w, out_0, out_1, out_2)
             nc.sync.dma_start(out=o_view[1][:, m, h * HW:(h + 1) * HW], in_=t[:, 0:HW])
             late_stores()
 
-        def membrane(k, widths, on_vector):
+        def membrane(k, on_vector):
             m, h = k % M_TILES, k // M_TILES
             t = pair[k]
             if k % 2 == 0:
                 spikes[k // 2] = grp.tile([P, 2 * HW], F32, name="spikes%d" % (k // 2), tag="grp", align_bytes=64)
             zt = spikes[k // 2]
             z0 = (k % 2) * HW
-            a = 0
-            for e, wid in enumerate(widths):
-                c0 = m * O + h * HW + a
-                ni = t[:, a:a + wid]
-                nv = t[:, HW + a:HW + a + wid]
-                nz = zt[:, z0 + a:z0 + a + wid]
+            c0 = m * O + h * HW
+            parts = range(0, HW, NT)
+            for a in parts:
                 nc.vector.scalar_tensor_tensor(
-                    out=nv, in0=v_sb[:, c0:c0 + wid], scalar=-BETA, in1=ni, op0=ALU.mult, op1=ALU.subtract)
+                    out=t[:, HW + a:HW + a + NT], in0=v_sb[:, c0 + a:c0 + a + NT], scalar=-BETA,
+                    in1=t[:, a:a + NT], op0=ALU.mult, op1=ALU.subtract)
+            for a in parts:
+                nv = t[:, HW + a:HW + a + NT]
                 nc.vector.scalar_tensor_tensor(
-                    out=nv, in0=z_sb[:, c0:c0 + wid], scalar=1.0, in1=nv, op0=ALU.subtract, op1=ALU.mult)
-                if on_vector and e == len(widths) - 1:
-                    nc.vector.tensor_scalar(out=nz, in0=nv, scalar1=1.0, scalar2=None, op0=ALU.is_gt)
-                else:
-                    nc.scalar.activation(out=nz, in_=nv, func=ACT.Relu, bias=neg_one[:], scale=1.0)
+                    out=nv, in0=z_sb[:, c0 + a:c0 + a + NT], scalar=1.0, in1=nv, op0=ALU.subtract, op1=ALU.mult)
+            if on_vector:
+                for a in parts:
+                    nc.vector.tensor_scalar(out=zt[:, z0 + a:z0 + a + NT], in0=t[:, HW + a:HW + a + NT],
+                                            scalar1=1.0, scalar2=None, op0=ALU.is_gt)
+            else:
+                for a in parts:
+                    nc.scalar.activation(out=zt[:, z0 + a:z0 + a + NT], in_=t[:, HW + a:HW + a + NT],
+                                         func=ACT.Relu, bias=neg_one[:], scale=1.0)
+                for a in parts:
+                    nz = zt[:, z0 + a:z0 + a + NT]
                     nc.scalar.activation(out=nz, in_=nz, func=ACT.Sign)
-                d0 = h * HW + a
-                nc.sync.dma_start(out=o_view[2][:, m, d0:d0 + wid], in_=nv)
-                if len(widths) > 1:
-                    late_stores()
-                late.append((o_view[0][:, m, d0:d0 + wid], nz))
-                a += wid
+            nc.sync.dma_start(out=o_view[2][:, m, h * HW:(h + 1) * HW], in_=t[:, HW:2 * HW])
+            late.append((o_view[0][:, m, h * HW:(h + 1) * HW], zt[:, z0:z0 + HW]))
 
         def second_half(m):
             for n in (2, 3):
@@ -276,10 +277,7 @@ def tile_liflayer_kernel(tc, inputs, I, V, Z, fwd_w, rec_w, out_0, out_1, out_2)
 
         for k in range(2 * M_TILES):
             current(k)
-            if k == 2 * M_TILES - 1:
-                membrane(k, LAST_PIECES, True)
-            else:
-                membrane(k, (HW,), False)
+            membrane(k, k == 2 * M_TILES - 1)
             if k < M_TILES:
                 flush()
                 second_half(k)

@@ -52,16 +52,7 @@ def tile_liflayer_kernel(tc, inputs, I, V, Z, fwd_w, rec_w, out_0, out_1, out_2)
             r0 = (c % 4) * 512
             t = big.tile([P, 4 * O], BF16, name="w%d" % c, tag="big")
             raw["w%d" % c] = t
-            halves = 2 if c == LAST else 1
-            wid = O // halves
-            for h in range(halves):
-                tv = t[:, h * 4 * wid:(h + 1) * 4 * wid].rearrange("p (t w) -> p t w", t=4)
-                for u in range(2):
-                    nc.sync.dma_start(
-                        out=tv[:, 2 * u:2 * u + 2, :],
-                        in_=src[r0 + 256 * u:r0 + 256 * (u + 1), h * wid:(h + 1) * wid].rearrange(
-                            "(q e) c -> q e c", e=2),
-                    )
+            nc.sync.dma_start(out=t[:], in_=src[r0:r0 + 512, :].rearrange("(q t) c -> q (t c)", t=4))
 
         def load_rows(t, src, mm):
             nc.sync.dma_start(out=t[:, 2 * mm * K:2 * (mm + 1) * K],
@@ -131,8 +122,8 @@ def tile_liflayer_kernel(tc, inputs, I, V, Z, fwd_w, rec_w, out_0, out_1, out_2)
                 xt = psum.tile([P, NT], F32, name="xt%d%d%d" % (s, mm, g), tag="bank")
                 for u in range(2):
                     for h in range(2):
-                        w0 = (2 * mm + h) * (K // 2) + 256 * g + 128 * u
-                        nc.tensor.transpose(xt[:, u * 256 + h * P:u * 256 + (h + 1) * P], srcf[:, w0:w0 + P], ident[:])
+                        w0 = (2 * mm + h) * (K // 2) + 256 * g + u
+                        nc.tensor.transpose(xt[:, u * 256 + h * P:u * 256 + (h + 1) * P], srcf[:, w0:w0 + 255:2], ident[:])
                 banks.append(xt)
             for g in range(4):
                 srcv = banks[g][:].rearrange("p (u b) -> p b u", u=2)
@@ -156,12 +147,8 @@ def tile_liflayer_kernel(tc, inputs, I, V, Z, fwd_w, rec_w, out_0, out_1, out_2)
         def w_step(j, engines):
             c, h = j // 2, j % 2
             gw = grp.tile([P, 4096], BF16, name="gw%d" % j, tag="grp", align_bytes=64)
-            if c == LAST:
-                rv = raw["w%d" % c][:, h * 4 * HW:(h + 1) * 4 * HW].rearrange("p (t w) -> p t w", t=4)
-                base = 0
-            else:
-                rv = raw["w%d" % c][:].rearrange("p (t w) -> p t w", t=4)
-                base = h * HW
+            rv = raw["w%d" % c][:].rearrange("p (t w) -> p t w", t=4)
+            base = h * HW
             for e in range(2):
                 dst = gw[:, e * 2048:(e + 1) * 2048].rearrange("p (c i t) -> p c t i", i=4, t=4)
                 srcv = rv[:, :, base + e * NT:base + (e + 1) * NT].rearrange("p t (c i) -> p c t i", i=4)
@@ -191,10 +178,18 @@ def tile_liflayer_kernel(tc, inputs, I, V, Z, fwd_w, rec_w, out_0, out_1, out_2)
             pending.append(finish)
 
         loads = list(ORDER) + [None, "iv"]
-        ahead = BIG_BUFS + 1
-        for item in loads[:ahead]:
-            load(item)
-        nxt = ahead
+        queue = list(loads)
+
+        def load_next():
+            while queue:
+                item = queue.pop(0)
+                if item is not None:
+                    load(item)
+                if item != "z":
+                    return
+
+        for i in range(BIG_BUFS):
+            load_next()
         for item in ORDER:
             if item == "w%d" % LAST:
                 w_step(2 * LAST, "vs")
@@ -208,10 +203,8 @@ def tile_liflayer_kernel(tc, inputs, I, V, Z, fwd_w, rec_w, out_0, out_1, out_2)
                 s = 0 if item == "x" else 1
                 act_step(s, 0)
                 act_step(s, 1)
-            if item != "z" and nxt < len(loads):
-                if loads[nxt] is not None:
-                    load(loads[nxt])
-                nxt += 1
+            if item != "z":
+                load_next()
         i_sb = raw["i"]
         v_sb = raw["v"]
         z_sb = raw["z"]

@@ -22,7 +22,7 @@ LAST = PASSES - 1
 ALPHA = math.exp(-0.001 / 0.01)
 BETA = math.exp(-0.001 / 0.005)
 FLOPS = 2 * 2 * B * K * O
-ORDER = ("w0", "x", "w1", "z", "w2", "w3", "w4", "w5", "w6", "w7")
+ORDER = ("w0", "w1", "x", "w2", "w3", "z", "w4", "w5", "w6", "w7")
 V_EXITS = (0,)
 BIG_BUFS = 4
 GRP_BUFS = 6

@@ -150,8 +150,8 @@ def tile_liflayer_kernel(tc, inputs, I, V, Z, fwd_w, rec_w, out_0, out_1, out_2)
             rv = raw["w%d" % c][:].rearrange("p (t w) -> p t w", t=4)
             base = h * HW
             for e in range(2):
-                dst = gw[:, e * 2048:(e + 1) * 2048].rearrange("p (c i t) -> p c t i", i=4, t=4)
-                srcv = rv[:, :, base + e * NT:base + (e + 1) * NT].rearrange("p t (c i) -> p c t i", i=4)
+                dst = gw[:, e * 2048:(e + 1) * 2048].rearrange("p (c i t) -> p c t i", i=8, t=4)
+                srcv = rv[:, :, base + e * NT:base + (e + 1) * NT].rearrange("p t (c i) -> p c t i", i=8)
                 if engines[e] == "v":
                     nc.vector.tensor_copy(out=dst, in_=srcv)
                 else:

@@ -212,13 +212,6 @@ def tile_liflayer_kernel(tc, inputs, I, V, Z, fwd_w, rec_w, out_0, out_1, out_2)
         o_view = [o.rearrange("(p j) c -> p j c", j=M_TILES) for o in (out_0, out_1, out_2)]
         pair = {}
         spikes = {}
-        late = []
-
-        def late_stores():
-            while late:
-                dst, srcv = late.pop(0)
-                nc.sync.dma_start(out=dst, in_=srcv)
-
         def current(k):
             m, h = k % M_TILES, k // M_TILES
             t = grp.tile([P, 2 * HW], F32, name="pair%d" % k, tag="grp", align_bytes=64)
@@ -229,7 +222,6 @@ def tile_liflayer_kernel(tc, inputs, I, V, Z, fwd_w, rec_w, out_0, out_1, out_2)
                     out=t[:, e * NT:(e + 1) * NT], in0=i_sb[:, c0:c0 + NT], scalar=ALPHA,
                     in1=acc[(m, 2 * h + e)][:], op0=ALU.mult, op1=ALU.add)
             nc.sync.dma_start(out=o_view[1][:, m, h * HW:(h + 1) * HW], in_=t[:, 0:HW])
-            late_stores()
 
         def membrane(k, on_vector):
             m, h = k % M_TILES, k // M_TILES
@@ -260,7 +252,7 @@ def tile_liflayer_kernel(tc, inputs, I, V, Z, fwd_w, rec_w, out_0, out_1, out_2)
                     nz = zt[:, z0 + a:z0 + a + NT]
                     nc.scalar.activation(out=nz, in_=nz, func=ACT.Sign)
             nc.sync.dma_start(out=o_view[2][:, m, h * HW:(h + 1) * HW], in_=t[:, HW:2 * HW])
-            late.append((o_view[0][:, m, h * HW:(h + 1) * HW], zt[:, z0:z0 + HW]))
+            (nc.sync if on_vector else nc.scalar).dma_start(out=o_view[0][:, m, h * HW:(h + 1) * HW], in_=zt[:, z0:z0 + HW])
 
         def second_half(m):
             for n in (2, 3):
@@ -274,4 +266,3 @@ def tile_liflayer_kernel(tc, inputs, I, V, Z, fwd_w, rec_w, out_0, out_1, out_2)
             if k < M_TILES:
                 flush()
                 second_half(k)
-        late_stores()

@@ -58,22 +58,24 @@ def tile_liflayer_kernel(tc, inputs, I, V, Z, fwd_w, rec_w, out_0, out_1, out_2)
             nc.sync.dma_start(out=t[:, 2 * mm * K:2 * (mm + 1) * K],
                               in_=src.rearrange("(p j) k -> p (j k)", j=M_TILES)[:, 2 * mm * K:2 * (mm + 1) * K])
 
+        def load_whole(t, src):
+            nc.sync.dma_start(out=t[:], in_=src.rearrange("(p j) k -> p (j k)", j=M_TILES))
+
         def load(item):
             if item[0] == "w":
                 load_w(int(item[1:]))
             elif item == "iv":
                 raw["i"] = big.tile([P, M_TILES * O], BF16, name="i_sb", tag="big")
                 raw["v"] = big.tile([P, M_TILES * O], BF16, name="v_sb", tag="big")
+                load_whole(raw["i"], I)
                 for mm in range(2):
-                    load_rows(raw["i"], I, mm)
                     load_rows(raw["v"], V, mm)
             else:
                 if item == "z":
                     raw[item] = keep.tile([P, M_TILES * K], BF16, name="z_sb")
                 else:
                     raw[item] = big.tile([P, M_TILES * K], BF16, name="x_sb", tag="big")
-                for mm in range(2):
-                    load_rows(raw[item], inputs if item == "x" else Z, mm)
+                load_whole(raw[item], inputs if item == "x" else Z)
 
         a_codes = {}
         a_scales = {}

@@ -22,8 +22,10 @@ LAST = PASSES - 1
 ALPHA = math.exp(-0.001 / 0.01)
 BETA = math.exp(-0.001 / 0.005)
 FLOPS = 2 * 2 * B * K * O
-ORDER = ("w0", "w1", "x", "w2", "w3", "z", "w4", "w5", "w6", "w7")
+ORDER = ("w0", "w1", "w2", "x", "w3", "z", "w4", "w5", "w6", "w7")
 V_EXITS = (0,)
+STEP_SCALE = 1.5 * 2.0 ** 36
+STEP_BIAS = STEP_SCALE + 2.0 ** 13
 BIG_BUFS = 4
 GRP_BUFS = 6
 
@@ -40,10 +42,10 @@ def tile_liflayer_kernel(tc, inputs, I, V, Z, fwd_w, rec_w, out_0, out_1, out_2)
 
         ident = const.tile([P, P], F32, name="ident")
         make_identity(nc, ident[:])
-        neg_one = const.tile([P, 1], F32, name="neg_one")
-        nc.vector.memset(neg_one[:], -1.0)
+        step_bias = const.tile([P, 1], F32, name="step_bias")
+        nc.vector.memset(step_bias[:], -STEP_BIAS)
         warm = const.tile([P, 1], F32, name="warm")
-        nc.scalar.activation(out=warm[:], in_=neg_one[:], func=ACT.Sign)
+        nc.scalar.activation(out=warm[:], in_=step_bias[:], func=ACT.Sigmoid)
 
         raw = {}
 
@@ -249,10 +251,7 @@ def tile_liflayer_kernel(tc, inputs, I, V, Z, fwd_w, rec_w, out_0, out_1, out_2)
             else:
                 for a in parts:
                     nc.scalar.activation(out=zt[:, z0 + a:z0 + a + NT], in_=t[:, HW + a:HW + a + NT],
-                                         func=ACT.Relu, bias=neg_one[:], scale=1.0)
-                for a in parts:
-                    nz = zt[:, z0 + a:z0 + a + NT]
-                    nc.scalar.activation(out=nz, in_=nz, func=ACT.Sign)
+                                         func=ACT.Sigmoid, bias=step_bias[:], scale=STEP_SCALE)
             nc.sync.dma_start(out=o_view[2][:, m, h * HW:(h + 1) * HW], in_=t[:, HW:2 * HW])
             (nc.sync if on_vector else nc.scalar).dma_start(out=o_view[0][:, m, h * HW:(h + 1) * HW], in_=zt[:, z0:z0 + HW])
 

import math
from contextlib import ExitStack

import concourse.mybir as mybir
from concourse.masks import make_identity

FP8X4 = mybir.dt.float8_e4m3fn_x4
BF16 = mybir.dt.bfloat16
F32 = mybir.dt.float32
U32 = mybir.dt.uint32
U8 = mybir.dt.uint8
ALU = mybir.AluOpType
ACT = mybir.ActivationFunctionType

P = 128
B, K, O = 512, 2048, 2048
NT = 512
HW = 1024
M_TILES = B // P
PASSES = 2 * K // 512
LAST = PASSES - 1
ALPHA = math.exp(-0.001 / 0.01)
BETA = math.exp(-0.001 / 0.005)
FLOPS = 2 * 2 * B * K * O
ORDER = ("w0", "w1", "w2", "x", "w3", "z", "w4", "w5", "w6", "w7")
V_EXITS = (0,)
STEP_SCALE = 1.5 * 2.0 ** 36
STEP_BIAS = STEP_SCALE + 2.0 ** 13
BIG_BUFS = 4
GRP_BUFS = 6


def tile_liflayer_kernel(tc, inputs, I, V, Z, fwd_w, rec_w, out_0, out_1, out_2):
    nc = tc.nc
    with ExitStack() as ctx:
        const = ctx.enter_context(tc.tile_pool(name="const", bufs=1))
        keep = ctx.enter_context(tc.tile_pool(name="keep", bufs=1))
        big = ctx.enter_context(tc.tile_pool(name="big", bufs=BIG_BUFS))
        grp = ctx.enter_context(tc.tile_pool(name="grp", bufs=GRP_BUFS))
        psum = ctx.enter_context(tc.psum_pool(name="psum", bufs=8))
        ctx.enter_context(tc.manual_schedule())

        ident = const.tile([P, P], F32, name="ident")
        make_identity(nc, ident[:])
        step_bias = const.tile([P, 1], F32, name="step_bias")
        nc.vector.memset(step_bias[:], -STEP_BIAS)
        warm = const.tile([P, 1], F32, name="warm")
        nc.scalar.activation(out=warm[:], in_=step_bias[:], func=ACT.Sigmoid)

        raw = {}

        def load_w(c):
            src = fwd_w if c < 4 else rec_w
            r0 = (c % 4) * 512
            t = big.tile([P, 4 * O], BF16, name="w%d" % c, tag="big")
            raw["w%d" % c] = t
            nc.sync.dma_start(out=t[:], in_=src[r0:r0 + 512, :].rearrange("(q t) c -> q (t c)", t=4))

        def load_rows(t, src, mm):
            nc.sync.dma_start(out=t[:, 2 * mm * K:2 * (mm + 1) * K],
                              in_=src.rearrange("(p j) k -> p (j k)", j=M_TILES)[:, 2 * mm * K:2 * (mm + 1) * K])

        def load_whole(t, src):
            nc.sync.dma_start(out=t[:], in_=src.rearrange("(p j) k -> p (j k)", j=M_TILES))

        def load(item):
            if item[0] == "w":
                load_w(int(item[1:]))
            elif item == "iv":
                raw["i"] = big.tile([P, M_TILES * O], BF16, name="i_sb", tag="big")
                raw["v"] = big.tile([P, M_TILES * O], BF16, name="v_sb", tag="big")
                load_whole(raw["i"], I)
                for mm in range(2):
                    load_rows(raw["v"], V, mm)
            else:
                if item == "z":
                    raw[item] = keep.tile([P, M_TILES * K], BF16, name="z_sb")
                else:
                    raw[item] = big.tile([P, M_TILES * K], BF16, name="x_sb", tag="big")
                load_whole(raw[item], inputs if item == "x" else Z)

        a_codes = {}
        a_scales = {}
        w_codes = {}
        w_scales = {}
        acc = {}
        pending = []
        pe_backlog = []
        split = []
        state = {"acts": 0}

        def mx_pass(m, n, c):
            s, g = c // 4, c % 4
            col = g * 256 + (m % 2) * P
            j = 2 * c + n // 2
            wcol = (n % 2) * NT
            nc.tensor.matmul_mx(
                out=acc[(m, n)][:],
                lhsT=a_codes[(s, m // 2)][:, col:col + P].bitcast(FP8X4),
                lhsT_scale=a_scales[(s, m // 2)][:, col:col + P],
                rhs=w_codes[j][:, wcol:wcol + NT].bitcast(FP8X4),
                rhs_scale=w_scales[j][:, wcol:wcol + NT],
                start=(c == 0),
                stop=(c == LAST),
            )

        def first_half_passes(c, ms):
            for m in ms:
                for n in range(2):
                    mx_pass(m, n, c)

        def flush():
            while pending:
                pending.pop(0)()

        def act_step(s, mm):
            srcf = raw["x" if s == 0 else "z"][:].bitcast(F32)
            codes = keep.tile([P, 4 * 256], U32, name="a_codes%d%d" % (s, mm), align_bytes=64)
            scales = keep.tile([P, 4 * 256], U8, name="a_scales%d%d" % (s, mm), align_bytes=64)
            a_codes[(s, mm)] = codes
            a_scales[(s, mm)] = scales
            ga = grp.tile([P, 4096], BF16, name="ga%d%d" % (s, mm), tag="grp", align_bytes=64)
            gaf = ga[:].bitcast(F32).rearrange("p (g b u) -> p g b u", g=4, u=2)
            banks = []
            for g in range(4):
                xt = psum.tile([P, NT], F32, name="xt%d%d%d" % (s, mm, g), tag="bank")
                for u in range(2):
                    for h in range(2):
                        w0 = (2 * mm + h) * (K // 2) + 256 * g + u
                        nc.tensor.transpose(xt[:, u * 256 + h * P:u * 256 + (h + 1) * P], srcf[:, w0:w0 + 255:2], ident[:])
                banks.append(xt)
            for g in range(4):
                srcv = banks[g][:].rearrange("p (u b) -> p b u", u=2)
                if g in V_EXITS:
                    nc.vector.tensor_copy(out=gaf[:, g, :, :], in_=srcv)
                else:
                    nc.scalar.copy(out=gaf[:, g, :, :], in_=srcv)
            flush()

            def finish():
                nc.vector.quantize_mx(out=codes[:].bitcast(FP8X4), scales=scales[:], in_=ga[:])
                state["acts"] += 1
                if state["acts"] == 4:
                    for n in range(2):
                        for m in range(M_TILES):
                            acc[(m, n)] = psum.tile([P, NT], F32, name="acc%d%d" % (m, n), tag="bank")
                    while pe_backlog:
                        first_half_passes(pe_backlog.pop(0), (0, 1, 2, 3))
            pending.append(finish)

        def w_step(j, engines):
            c, h = j // 2, j % 2
            gw = grp.tile([P, 4096], BF16, name="gw%d" % j, tag="grp", align_bytes=64)
            rv = raw["w%d" % c][:].rearrange("p (t w) -> p t w", t=4)
            base = h * HW
            for e in range(2):
                dst = gw[:, e * 2048:(e + 1) * 2048].rearrange("p (c i t) -> p c t i", i=8, t=4)
                srcv = rv[:, :, base + e * NT:base + (e + 1) * NT].rearrange("p t (c i) -> p c t i", i=8)
                if engines[e] == "v":
                    nc.vector.tensor_copy(out=dst, in_=srcv)
                else:
                    nc.scalar.copy(out=dst, in_=srcv)
            flush()

            def finish():
                codes = keep.tile([P, 2 * NT], U32, name="w_codes%d" % j, align_bytes=64)
                scales = keep.tile([P, 2 * NT], U8, name="w_scales%d" % j, align_bytes=64)
                w_codes[j] = codes
                w_scales[j] = scales
                nc.vector.quantize_mx(out=codes[:].bitcast(FP8X4), scales=scales[:], in_=gw[:])
                if state["acts"] < 4:
                    if h == 0:
                        pe_backlog.append(c)
                elif c == LAST:
                    if h == 0:
                        first_half_passes(c, (0, 1, 2, 3))
                elif c in split:
                    first_half_passes(c, (2, 3))
                elif h == 0:
                    first_half_passes(c, (0, 1))
                    split.append(c)
            pending.append(finish)

        loads = list(ORDER) + [None, "iv"]
        queue = list(loads)

        def load_next():
            while queue:
                item = queue.pop(0)
                if item is not None:
                    load(item)
                if item != "z":
                    return

        for i in range(BIG_BUFS):
            load_next()
        for item in ORDER:
            if item == "w%d" % LAST:
                w_step(2 * LAST, "vs")
                flush()
                w_step(2 * LAST + 1, "ss")
            elif item[0] == "w":
                c = int(item[1:])
                w_step(2 * c, "vs")
                w_step(2 * c + 1, "vs")
            else:
                s = 0 if item == "x" else 1
                act_step(s, 0)
                act_step(s, 1)
            if item != "z":
                load_next()
        i_sb = raw["i"]
        v_sb = raw["v"]
        z_sb = raw["z"]

        o_view = [o.rearrange("(p j) c -> p j c", j=M_TILES) for o in (out_0, out_1, out_2)]
        pair = {}
        spikes = {}
        def current(k):
            m, h = k % M_TILES, k // M_TILES
            t = grp.tile([P, 2 * HW], F32, name="pair%d" % k, tag="grp", align_bytes=64)
            pair[k] = t
            for e in range(2):
                c0 = m * O + h * HW + e * NT
                nc.vector.scalar_tensor_tensor(
                    out=t[:, e * NT:(e + 1) * NT], in0=i_sb[:, c0:c0 + NT], scalar=ALPHA,
                    in1=acc[(m, 2 * h + e)][:], op0=ALU.mult, op1=ALU.add)
            nc.sync.dma_start(out=o_view[1][:, m, h * HW:(h + 1) * HW], in_=t[:, 0:HW])

        def membrane(k, on_vector):
            m, h = k % M_TILES, k // M_TILES
            t = pair[k]
            if k % 2 == 0:
                spikes[k // 2] = grp.tile([P, 2 * HW], F32, name="spikes%d" % (k // 2), tag="grp", align_bytes=64)
            zt = spikes[k // 2]
            z0 = (k % 2) * HW
            c0 = m * O + h * HW
            parts = range(0, HW, NT)
            for a in parts:
                nc.vector.scalar_tensor_tensor(
                    out=t[:, HW + a:HW + a + NT], in0=v_sb[:, c0 + a:c0 + a + NT], scalar=-BETA,
                    in1=t[:, a:a + NT], op0=ALU.mult, op1=ALU.subtract)
            for a in parts:
                nv = t[:, HW + a:HW + a + NT]
                nc.vector.scalar_tensor_tensor(
                    out=nv, in0=z_sb[:, c0 + a:c0 + a + NT], scalar=1.0, in1=nv, op0=ALU.subtract, op1=ALU.mult)
            if on_vector:
                for a in parts:
                    nc.vector.tensor_scalar(out=zt[:, z0 + a:z0 + a + NT], in0=t[:, HW + a:HW + a + NT],
                                            scalar1=1.0, scalar2=None, op0=ALU.is_gt)
            else:
                for a in parts:
                    nc.scalar.activation(out=zt[:, z0 + a:z0 + a + NT], in_=t[:, HW + a:HW + a + NT],
                                         func=ACT.Sigmoid, bias=step_bias[:], scale=STEP_SCALE)
            nc.sync.dma_start(out=o_view[2][:, m, h * HW:(h + 1) * HW], in_=t[:, HW:2 * HW])
            (nc.sync if on_vector else nc.scalar).dma_start(out=o_view[0][:, m, h * HW:(h + 1) * HW], in_=zt[:, z0:z0 + HW])

        def second_half(m):
            for n in (2, 3):
                acc[(m, n)] = psum.tile([P, NT], F32, name="acc%d%d" % (m, n), tag="bank")
                for c in range(PASSES):
                    mx_pass(m, n, c)

        for k in range(2 * M_TILES):
            current(k)
            membrane(k, k == 2 * M_TILES - 1)
            if k < M_TILES:
                flush()
                second_half(k)
